import numpy as np
import ml_dtypes


def mxq(x, axis, fmt="e4m3"):
    dtype, down = {"e4m3": (ml_dtypes.float8_e4m3fn, 7), "e5m2": (ml_dtypes.float8_e5m2, 14)}[fmt]
    v = np.moveaxis(np.asarray(x, np.float32).astype(ml_dtypes.bfloat16).astype(np.float64), axis, -1)
    blocks = v.reshape(v.shape[:-1] + (-1, 32))
    amax = np.abs(blocks).max(-1, keepdims=True)
    byte = np.maximum(np.where(amax > 0, np.frexp(amax)[1] - 1 + 127, 0) - down, 1)
    scale = np.exp2(byte - 127.0)
    codes = (blocks / scale).astype(np.float32).astype(dtype).astype(np.float64)
    return np.moveaxis((codes * scale).reshape(v.shape), -1, axis)


WIDE = False


def mx_kscale(k):
    if not WIDE:
        return np.ones(k)
    levels = np.array([10, -10, 5, -5, 0])
    a = np.random.permutation(np.resize(levels, k // 512 * 4)).reshape(k // 512, 4)
    idx = np.arange(k)
    return np.exp2(a[idx // 512, idx % 128 // 32])


BF16 = ml_dtypes.bfloat16


def bf(x):
    return np.asarray(x, np.float32).astype(BF16)


def f64(x):
    return np.asarray(x).astype(np.float64)


N, G, F, K, E = 4096, 128, 128, 4, 1


def setup_inputs():
    s = mx_kscale(N)
    return {"x": bf(np.random.standard_normal((N, G)) * s[:, None]),
            "S": bf(np.random.standard_normal((E, N, N)) / np.sqrt(N) / s[:, None] * s[None, :])}


def reference(x, S):
    Sq = mxq(f64(S), 1, "e4m3")
    z0 = np.broadcast_to(f64(x).T[None], (E, G, N))
    z1 = mxq(z0, 2, "e4m3") @ Sq
    z2 = mxq(z1, 2, "e4m3") @ Sq
    return z1, z2

@@ -1,0 +1,198 @@
+from contextlib import ExitStack
+
+import concourse.mybir as mybir
+from concourse.masks import make_identity
+
+FP8X4 = mybir.dt.float8_e4m3fn_x4
+BF16 = mybir.dt.bfloat16
+F32 = mybir.dt.float32
+U32 = mybir.dt.uint32
+U8 = mybir.dt.uint8
+
+P = 128
+NODES = 4096
+FEAT = 128
+PACK = 4
+K_PASS = P * PACK
+PASSES = NODES // K_PASS
+BANK_W = 512
+GROUP_W = 1024
+GROUPS = NODES // GROUP_W
+J_PER_GROUP = GROUP_W // BANK_W
+
+FLOPS = 2 * 2 * FEAT * NODES * NODES
+
+
+def tile_graphfilter_pa_kernel(tc, x, S, out_0, out_1):
+    nc = tc.nc
+    with ExitStack() as ctx:
+        keep = ctx.enter_context(tc.tile_pool(name="keep", bufs=1))
+        rawp = ctx.enter_context(tc.tile_pool(name="rawp", bufs=4))
+        grp = ctx.enter_context(tc.tile_pool(name="grp", bufs=2))
+        zp = ctx.enter_context(tc.tile_pool(name="zp", bufs=2))
+        psum = ctx.enter_context(tc.psum_pool(name="psum", bufs=1))
+
+        ident = keep.tile([P, P], F32, name="ident")
+        make_identity(nc, ident[:])
+
+        xraw = rawp.tile([P, PASSES, PACK * FEAT], BF16, name="xraw", tag="raw")
+        nc.sync.dma_start(out=xraw[:], in_=x.rearrange("(c p t) g -> p c (t g)", p=P, t=PACK))
+        xq_codes = keep.tile([P, PASSES * FEAT], U32, name="xq_codes", align_bytes=64)
+        xq_scales = keep.tile([P, PASSES * FEAT], U8, name="xq_scales", align_bytes=64)
+        half = PASSES // 2
+        xg_a = grp.tile([P, half * FEAT * PACK], BF16, name="xg_a", tag="gv", align_bytes=64)
+        xg_b = grp.tile([P, half * FEAT * PACK], BF16, name="xg_b", tag="gs", align_bytes=64)
+        nc.vector.tensor_copy(
+            out=xg_a[:].rearrange("p (c g t) -> p c g t", c=half, t=PACK),
+            in_=xraw[:, 0:half, :].rearrange("p c (t g) -> p c g t", t=PACK),
+        )
+        nc.scalar.copy(
+            out=xg_b[:].rearrange("p (c g t) -> p c g t", c=half, t=PACK),
+            in_=xraw[:, half:PASSES, :].rearrange("p c (t g) -> p c g t", t=PACK),
+        )
+        hw = half * FEAT
+        nc.vector.quantize_mx(out=xq_codes[:, 0:hw].bitcast(FP8X4), scales=xq_scales[:, 0:hw], in_=xg_a[:])
+        nc.vector.quantize_mx(
+            out=xq_codes[:, hw : 2 * hw].bitcast(FP8X4), scales=xq_scales[:, hw : 2 * hw], in_=xg_b[:]
+        )
+
+        s_codes = {}
+        s_scales = {}
+        z1q_codes = {}
+        z1q_scales = {}
+        acc = {}
+
+        def s_operand(c, j):
+            g = j // J_PER_GROUP
+            lo = (j % J_PER_GROUP) * BANK_W
+            return (
+                s_codes[(c, g)][:, lo : lo + BANK_W].bitcast(FP8X4),
+                s_scales[(c, g)][:, lo : lo + BANK_W],
+            )
+
+        def open_group(key, tag, total):
+            acc[key] = [psum.tile([P, BANK_W], F32, name="acc_%s" % key, tag=tag), 0, total]
+
+        def mx_pass(key, lhs_codes, lhs_scales, c, j):
+            entry = acc[key]
+            rhs, rhs_scale = s_operand(c, j)
+            nc.tensor.matmul_mx(
+                out=entry[0][:],
+                lhsT=lhs_codes.bitcast(FP8X4),
+                lhsT_scale=lhs_scales,
+                rhs=rhs,
+                rhs_scale=rhs_scale,
+                start=(entry[1] == 0),
+                stop=(entry[1] == entry[2] - 1),
+            )
+            entry[1] = entry[1] + 1
+
+        def z1_pass(c, j):
+            mx_pass("z1_%d" % j, xq_codes[:, c * FEAT : (c + 1) * FEAT], xq_scales[:, c * FEAT : (c + 1) * FEAT], c, j)
+
+        def z2_pass(key, c, j):
+            g = c // J_PER_GROUP
+            lo = (c % J_PER_GROUP) * FEAT
+            mx_pass(key, z1q_codes[g][:, lo : lo + FEAT], z1q_scales[g][:, lo : lo + FEAT], c, j)
+
+        z2_tag = {0: "b4", 1: "b5", 2: "b6", 3: "b7", 4: "b2", 5: "b3", 6: "b4", 7: "b5"}
+        spill = {}
+
+        for g in range(GROUPS):
+            js = [g * J_PER_GROUP + i for i in range(J_PER_GROUP)]
+            for i in range(J_PER_GROUP):
+                open_group("z1_%d" % js[i], "b%d" % i, PASSES)
+            for j in js:
+                if g > 0:
+                    open_group("z2_%d" % j, z2_tag[j], PASSES)
+            for c in range(PASSES):
+                raw = rawp.tile([P, PACK, GROUP_W], BF16, name="raw", tag="raw")
+                nc.sync.dma_start(
+                    out=raw[:],
+                    in_=S[0, c * K_PASS : (c + 1) * K_PASS, g * GROUP_W : (g + 1) * GROUP_W].rearrange(
+                        "(p t) w -> p t w", t=PACK
+                    ),
+                )
+                gv = grp.tile([P, BANK_W * PACK], BF16, name="gv", tag="gv", align_bytes=64)
+                gs = grp.tile([P, BANK_W * PACK], BF16, name="gs", tag="gs", align_bytes=64)
+                nc.vector.tensor_copy(
+                    out=gv[:].rearrange("p (c i t) -> p c t i", i=4, t=PACK),
+                    in_=raw[:, :, 0:BANK_W].rearrange("p t (c i) -> p c t i", i=4),
+                )
+                nc.scalar.copy(
+                    out=gs[:].rearrange("p (c i t) -> p c t i", i=4, t=PACK),
+                    in_=raw[:, :, BANK_W:GROUP_W].rearrange("p t (c i) -> p c t i", i=4),
+                )
+                codes = keep.tile([P, GROUP_W], U32, name="sc_%d_%d" % (c, g), align_bytes=64)
+                scales = keep.tile([P, GROUP_W], U8, name="ss_%d_%d" % (c, g), align_bytes=64)
+                s_codes[(c, g)] = codes
+                s_scales[(c, g)] = scales
+                nc.vector.quantize_mx(out=codes[:, 0:BANK_W].bitcast(FP8X4), scales=scales[:, 0:BANK_W], in_=gv[:])
+                nc.vector.quantize_mx(
+                    out=codes[:, BANK_W:GROUP_W].bitcast(FP8X4), scales=scales[:, BANK_W:GROUP_W], in_=gs[:]
+                )
+                for j in js:
+                    z1_pass(c, j)
+                if c < g * J_PER_GROUP:
+                    for j in js:
+                        z2_pass("z2_%d" % j, c, j)
+
+            z1sb = zp.tile([P, GROUP_W], F32, name="z1sb")
+            nc.scalar.copy(out=z1sb[:, 0:BANK_W], in_=acc["z1_%d" % js[0]][0][:])
+            if g == GROUPS - 1:
+                nc.vector.tensor_copy(out=z1sb[:, BANK_W:GROUP_W], in_=acc["z1_%d" % js[1]][0][:])
+            else:
+                nc.scalar.copy(out=z1sb[:, BANK_W:GROUP_W], in_=acc["z1_%d" % js[1]][0][:])
+            nc.sync.dma_start(out=out_0[0, :, g * GROUP_W : (g + 1) * GROUP_W], in_=z1sb[:])
+            z1tg = zp.tile([P, J_PER_GROUP * FEAT * PACK], BF16, name="z1tg", bufs=1, align_bytes=64)
+            zts = []
+            for i in range(J_PER_GROUP):
+                zt = psum.tile([P, PACK, FEAT], F32, name="zt", tag=("b%d" % (2 + i) if g < 2 else "b%d" % i))
+                zts.append(zt)
+                view = z1sb[:, i * BANK_W : (i + 1) * BANK_W].rearrange("f (p t) -> f t p", t=PACK)
+                for t in range(PACK):
+                    nc.tensor.transpose(zt[:, t, :], view[:, t, :], ident[:])
+            w = FEAT * PACK
+            nc.vector.tensor_copy(
+                out=z1tg[:, 0:w].rearrange("p (f t) -> p f t", t=PACK), in_=zts[0][:].rearrange("p t f -> p f t")
+            )
+            nc.scalar.copy(
+                out=z1tg[:, w : 2 * w].rearrange("p (f t) -> p f t", t=PACK), in_=zts[1][:].rearrange("p t f -> p f t")
+            )
+            zc = keep.tile([P, J_PER_GROUP * FEAT], U32, name="z1qc_%d" % g, align_bytes=64)
+            zs = keep.tile([P, J_PER_GROUP * FEAT], U8, name="z1qs_%d" % g, align_bytes=64)
+            z1q_codes[g] = zc
+            z1q_scales[g] = zs
+            nc.vector.quantize_mx(out=zc[:].bitcast(FP8X4), scales=zs[:], in_=z1tg[:])
+
+            if g == 0:
+                for j in js:
+                    open_group("z2_%d" % j, z2_tag[j], 6)
+            if g < GROUPS - 1:
+                for j in range((g + 1) * J_PER_GROUP):
+                    for c in js:
+                        z2_pass("z2_%d" % j, c, j)
+            if g == GROUPS - 2:
+                for j in range(2):
+                    sp = keep.tile([P, BANK_W], F32, name="spill_%d" % j)
+                    spill[j] = sp
+                    nc.scalar.copy(out=sp[:], in_=acc["z2_%d" % j][0][:])
+
+        last = [6, 7]
+        z2sb = [rawp.tile([P, 4 * BANK_W], F32, name="z2sb_%d" % h, tag="raw") for h in range(2)]
+        order = [2, 3, 4, 5, 6, 7, 0, 1]
+        for n, j in enumerate(order):
+            key = "z2_%d" % j
+            if j < 2:
+                key = "z2b_%d" % j
+                open_group(key, "b%d" % j, 2)
+            for c in last:
+                z2_pass(key, c, j)
+            dst = z2sb[j // 4][:, (j % 4) * BANK_W : (j % 4 + 1) * BANK_W]
+            if j < 2:
+                nc.vector.tensor_tensor(out=dst, in0=acc[key][0][:], in1=spill[j][:], op=mybir.AluOpType.add)
+            elif n % 2 == 0:
+                nc.vector.tensor_copy(out=dst, in_=acc[key][0][:])
+            else:
+                nc.scalar.copy(out=dst, in_=acc[key][0][:])
+            nc.sync.dma_start(out=out_1[0, :, j * BANK_W : (j + 1) * BANK_W], in_=dst)

@@ -18,7 +18,15 @@ PASSES = NODES // K_PASS
 BANK_W = 512
 GROUP_W = 1024
 GROUPS = NODES // GROUP_W
-J_PER_GROUP = GROUP_W // BANK_W
+JPG = GROUP_W // BANK_W
+CHUNKS = GROUPS * PASSES
+RAW_BUFS = 4
+FILL_KEEP = 6
+CUT = 344
+FA = 2
+FB = 1
+FC = 1
+AHEAD = 2
 
 FLOPS = 2 * 2 * FEAT * NODES * NODES
 
@@ -26,62 +34,88 @@ FLOPS = 2 * 2 * FEAT * NODES * NODES
 def tile_graphfilter_pa_kernel(tc, x, S, out_0, out_1):
     nc = tc.nc
     with ExitStack() as ctx:
+        ctx.enter_context(tc.manual_schedule())
         keep = ctx.enter_context(tc.tile_pool(name="keep", bufs=1))
-        rawp = ctx.enter_context(tc.tile_pool(name="rawp", bufs=4))
+        rawp = ctx.enter_context(tc.tile_pool(name="rawp", bufs=RAW_BUFS))
         grp = ctx.enter_context(tc.tile_pool(name="grp", bufs=2))
-        zp = ctx.enter_context(tc.tile_pool(name="zp", bufs=2))
         psum = ctx.enter_context(tc.psum_pool(name="psum", bufs=1))
 
         ident = keep.tile([P, P], F32, name="ident")
         make_identity(nc, ident[:])
 
-        xraw = rawp.tile([P, PASSES, PACK * FEAT], BF16, name="xraw", tag="raw")
-        nc.sync.dma_start(out=xraw[:], in_=x.rearrange("(c p t) g -> p c (t g)", p=P, t=PACK))
-        xq_codes = keep.tile([P, PASSES * FEAT], U32, name="xq_codes", align_bytes=64)
-        xq_scales = keep.tile([P, PASSES * FEAT], U8, name="xq_scales", align_bytes=64)
-        half = PASSES // 2
-        xg_a = grp.tile([P, half * FEAT * PACK], BF16, name="xg_a", tag="gv", align_bytes=64)
-        xg_b = grp.tile([P, half * FEAT * PACK], BF16, name="xg_b", tag="gs", align_bytes=64)
-        nc.vector.tensor_copy(
-            out=xg_a[:].rearrange("p (c g t) -> p c g t", c=half, t=PACK),
-            in_=xraw[:, 0:half, :].rearrange("p c (t g) -> p c g t", t=PACK),
-        )
-        nc.scalar.copy(
-            out=xg_b[:].rearrange("p (c g t) -> p c g t", c=half, t=PACK),
-            in_=xraw[:, half:PASSES, :].rearrange("p c (t g) -> p c g t", t=PACK),
-        )
-        hw = half * FEAT
-        nc.vector.quantize_mx(out=xq_codes[:, 0:hw].bitcast(FP8X4), scales=xq_scales[:, 0:hw], in_=xg_a[:])
-        nc.vector.quantize_mx(
-            out=xq_codes[:, hw : 2 * hw].bitcast(FP8X4), scales=xq_scales[:, hw : 2 * hw], in_=xg_b[:]
-        )
-
+        raws = {}
+        grouped = {}
         s_codes = {}
         s_scales = {}
         z1q_codes = {}
         z1q_scales = {}
+        z1sb = {}
+        zts = {}
+        z1tg = {}
         acc = {}
+        spill = {}
 
-        def s_operand(c, j):
-            g = j // J_PER_GROUP
-            lo = (j % J_PER_GROUP) * BANK_W
-            return (
-                s_codes[(c, g)][:, lo : lo + BANK_W].bitcast(FP8X4),
-                s_scales[(c, g)][:, lo : lo + BANK_W],
+        def load(n):
+            g, c = divmod(n, PASSES)
+            raw = rawp.tile([P, PACK, GROUP_W], BF16, name="raw", tag="raw")
+            raws[n] = raw
+            nc.sync.dma_start(
+                out=raw[:],
+                in_=S[0, c * K_PASS : (c + 1) * K_PASS, g * GROUP_W : (g + 1) * GROUP_W].rearrange(
+                    "(p t) w -> p t w", t=PACK
+                ),
             )
+
+        def regroup_part(engine_copy, dst, src):
+            engine_copy(
+                out=dst.rearrange("p (c i t) -> p c t i", i=4, t=PACK),
+                in_=src.rearrange("p t (c i) -> p c t i", i=4),
+            )
+
+        def regroup(n):
+            raw = raws[n]
+            gv = grp.tile([P, BANK_W * PACK], BF16, name="gv", tag="gv", align_bytes=64)
+            gs = grp.tile([P, BANK_W * PACK], BF16, name="gs", tag="gs", align_bytes=64)
+            grouped[n] = (gv, gs)
+            regroup_part(nc.vector.tensor_copy, gv[:], raw[:, :, 0:BANK_W])
+            regroup_part(nc.scalar.copy, gs[:], raw[:, :, BANK_W:GROUP_W])
+
+        def regroup_last(n, cut):
+            raw = raws[n]
+            gv = grp.tile([P, BANK_W * PACK], BF16, name="gv", tag="gv", align_bytes=64)
+            gs = grp.tile([P, BANK_W * PACK], BF16, name="gs", tag="gs", align_bytes=64)
+            grouped[n] = (gv, gs)
+            for h, dst in enumerate((gv, gs)):
+                lo = h * BANK_W
+                regroup_part(nc.vector.tensor_copy, dst[:, 0 : cut * PACK], raw[:, :, lo : lo + cut])
+                regroup_part(nc.scalar.copy, dst[:, cut * PACK : BANK_W * PACK], raw[:, :, lo + cut : lo + BANK_W])
+
+        def quantise(n, halves=(0, 1)):
+            g, c = divmod(n, PASSES)
+            if (c, g) not in s_codes:
+                s_codes[(c, g)] = keep.tile([P, GROUP_W], U32, name="sc_%d_%d" % (c, g), align_bytes=64)
+                s_scales[(c, g)] = keep.tile([P, GROUP_W], U8, name="ss_%d_%d" % (c, g), align_bytes=64)
+            for h in halves:
+                lo = h * BANK_W
+                nc.vector.quantize_mx(
+                    out=s_codes[(c, g)][:, lo : lo + BANK_W].bitcast(FP8X4),
+                    scales=s_scales[(c, g)][:, lo : lo + BANK_W],
+                    in_=grouped[n][h][:],
+                )
 
         def open_group(key, tag, total):
             acc[key] = [psum.tile([P, BANK_W], F32, name="acc_%s" % key, tag=tag), 0, total]
 
         def mx_pass(key, lhs_codes, lhs_scales, c, j):
             entry = acc[key]
-            rhs, rhs_scale = s_operand(c, j)
+            g = j // JPG
+            lo = (j % JPG) * BANK_W
             nc.tensor.matmul_mx(
                 out=entry[0][:],
                 lhsT=lhs_codes.bitcast(FP8X4),
                 lhsT_scale=lhs_scales,
-                rhs=rhs,
-                rhs_scale=rhs_scale,
+                rhs=s_codes[(c, g)][:, lo : lo + BANK_W].bitcast(FP8X4),
+                rhs_scale=s_scales[(c, g)][:, lo : lo + BANK_W],
                 start=(entry[1] == 0),
                 stop=(entry[1] == entry[2] - 1),
             )
@@ -91,108 +125,173 @@ def tile_graphfilter_pa_kernel(tc, x, S, out_0, out_1):
             mx_pass("z1_%d" % j, xq_codes[:, c * FEAT : (c + 1) * FEAT], xq_scales[:, c * FEAT : (c + 1) * FEAT], c, j)
 
         def z2_pass(key, c, j):
-            g = c // J_PER_GROUP
-            lo = (c % J_PER_GROUP) * FEAT
-            mx_pass(key, z1q_codes[g][:, lo : lo + FEAT], z1q_scales[g][:, lo : lo + FEAT], c, j)
+            mx_pass(key, z1q_codes[c][:], z1q_scales[c][:], c, j)
 
         z2_tag = {0: "b4", 1: "b5", 2: "b6", 3: "b7", 4: "b2", 5: "b3", 6: "b4", 7: "b5"}
-        spill = {}
 
-        for g in range(GROUPS):
-            js = [g * J_PER_GROUP + i for i in range(J_PER_GROUP)]
-            for i in range(J_PER_GROUP):
-                open_group("z1_%d" % js[i], "b%d" % i, PASSES)
+        def evac_z1(engine_copy, j):
+            g = j // JPG
+            if g not in z1sb:
+                if g == GROUPS - 1:
+                    z1sb[g] = rawp.tile([P, GROUP_W], F32, name="z1sb_last", tag="raw")
+                else:
+                    z1sb[g] = keep.tile([P, GROUP_W], F32, name="z1sb_%d" % g)
+            lo = (j % JPG) * BANK_W
+            engine_copy(out=z1sb[g][:, lo : lo + BANK_W], in_=acc["z1_%d" % j][0][:])
+
+        def transposes(j):
+            g = j // JPG
+            i = j % JPG
+            zt = psum.tile([P, PACK, FEAT], F32, name="zt", tag=("b%d" % (2 + i) if g < 2 else "b%d" % i))
+            zts[j] = zt
+            view = z1sb[g][:, i * BANK_W : (i + 1) * BANK_W].rearrange("f (p t) -> f t p", t=PACK)
+            for t in range(PACK):
+                nc.tensor.transpose(zt[:, t, :], view[:, t, :], ident[:])
+
+        def evac_zt(engine_copy, j):
+            tg = keep.tile([P, FEAT * PACK], BF16, name="z1tg", tag="z1tg%d" % (j % JPG), align_bytes=64)
+            z1tg[j] = tg
+            engine_copy(out=tg[:].rearrange("p (f t) -> p f t", t=PACK), in_=zts[j][:].rearrange("p t f -> p f t"))
+
+        def quantise_z1(j):
+            z1q_codes[j] = keep.tile([P, FEAT], U32, name="z1qc_%d" % j, align_bytes=64)
+            z1q_scales[j] = keep.tile([P, FEAT], U8, name="z1qs_%d" % j, align_bytes=64)
+            nc.vector.quantize_mx(out=z1q_codes[j][:].bitcast(FP8X4), scales=z1q_scales[j][:], in_=z1tg[j][:])
+
+        state = {"waiting": [], "held": []}
+
+        def stream_passes(n):
+            g, c = divmod(n, PASSES)
+            js = [g * JPG + i for i in range(JPG)]
+            if c == 0:
+                for i in range(JPG):
+                    open_group("z1_%d" % js[i], "b%d" % i, PASSES)
             for j in js:
-                if g > 0:
-                    open_group("z2_%d" % j, z2_tag[j], PASSES)
-            for c in range(PASSES):
-                raw = rawp.tile([P, PACK, GROUP_W], BF16, name="raw", tag="raw")
-                nc.sync.dma_start(
-                    out=raw[:],
-                    in_=S[0, c * K_PASS : (c + 1) * K_PASS, g * GROUP_W : (g + 1) * GROUP_W].rearrange(
-                        "(p t) w -> p t w", t=PACK
-                    ),
-                )
-                gv = grp.tile([P, BANK_W * PACK], BF16, name="gv", tag="gv", align_bytes=64)
-                gs = grp.tile([P, BANK_W * PACK], BF16, name="gs", tag="gs", align_bytes=64)
-                nc.vector.tensor_copy(
-                    out=gv[:].rearrange("p (c i t) -> p c t i", i=4, t=PACK),
-                    in_=raw[:, :, 0:BANK_W].rearrange("p t (c i) -> p c t i", i=4),
-                )
-                nc.scalar.copy(
-                    out=gs[:].rearrange("p (c i t) -> p c t i", i=4, t=PACK),
-                    in_=raw[:, :, BANK_W:GROUP_W].rearrange("p t (c i) -> p c t i", i=4),
-                )
-                codes = keep.tile([P, GROUP_W], U32, name="sc_%d_%d" % (c, g), align_bytes=64)
-                scales = keep.tile([P, GROUP_W], U8, name="ss_%d_%d" % (c, g), align_bytes=64)
-                s_codes[(c, g)] = codes
-                s_scales[(c, g)] = scales
-                nc.vector.quantize_mx(out=codes[:, 0:BANK_W].bitcast(FP8X4), scales=scales[:, 0:BANK_W], in_=gv[:])
-                nc.vector.quantize_mx(
-                    out=codes[:, BANK_W:GROUP_W].bitcast(FP8X4), scales=scales[:, BANK_W:GROUP_W], in_=gs[:]
-                )
+                z1_pass(c, j)
+            if c < g * JPG:
                 for j in js:
-                    z1_pass(c, j)
-                if c < g * J_PER_GROUP:
-                    for j in js:
-                        z2_pass("z2_%d" % j, c, j)
+                    state["waiting"].append((c, j))
 
-            z1sb = zp.tile([P, GROUP_W], F32, name="z1sb")
-            nc.scalar.copy(out=z1sb[:, 0:BANK_W], in_=acc["z1_%d" % js[0]][0][:])
-            if g == GROUPS - 1:
-                nc.vector.tensor_copy(out=z1sb[:, BANK_W:GROUP_W], in_=acc["z1_%d" % js[1]][0][:])
-            else:
-                nc.scalar.copy(out=z1sb[:, BANK_W:GROUP_W], in_=acc["z1_%d" % js[1]][0][:])
-            nc.sync.dma_start(out=out_0[0, :, g * GROUP_W : (g + 1) * GROUP_W], in_=z1sb[:])
-            z1tg = zp.tile([P, J_PER_GROUP * FEAT * PACK], BF16, name="z1tg", bufs=1, align_bytes=64)
-            zts = []
-            for i in range(J_PER_GROUP):
-                zt = psum.tile([P, PACK, FEAT], F32, name="zt", tag=("b%d" % (2 + i) if g < 2 else "b%d" % i))
-                zts.append(zt)
-                view = z1sb[:, i * BANK_W : (i + 1) * BANK_W].rearrange("f (p t) -> f t p", t=PACK)
-                for t in range(PACK):
-                    nc.tensor.transpose(zt[:, t, :], view[:, t, :], ident[:])
-            w = FEAT * PACK
-            nc.vector.tensor_copy(
-                out=z1tg[:, 0:w].rearrange("p (f t) -> p f t", t=PACK), in_=zts[0][:].rearrange("p t f -> p f t")
-            )
-            nc.scalar.copy(
-                out=z1tg[:, w : 2 * w].rearrange("p (f t) -> p f t", t=PACK), in_=zts[1][:].rearrange("p t f -> p f t")
-            )
-            zc = keep.tile([P, J_PER_GROUP * FEAT], U32, name="z1qc_%d" % g, align_bytes=64)
-            zs = keep.tile([P, J_PER_GROUP * FEAT], U8, name="z1qs_%d" % g, align_bytes=64)
-            z1q_codes[g] = zc
-            z1q_scales[g] = zs
-            nc.vector.quantize_mx(out=zc[:].bitcast(FP8X4), scales=zs[:], in_=z1tg[:])
+        def waiting_passes(count=99):
+            for c, j in state["waiting"][0:count]:
+                if "z2_%d" % j not in acc:
+                    open_group("z2_%d" % j, z2_tag[j], PASSES)
+                z2_pass("z2_%d" % j, c, j)
+            state["waiting"] = state["waiting"][count:]
 
+        def group_passes(g):
+            js = [g * JPG + i for i in range(JPG)]
             if g == 0:
                 for j in js:
                     open_group("z2_%d" % j, z2_tag[j], 6)
-            if g < GROUPS - 1:
-                for j in range((g + 1) * J_PER_GROUP):
-                    for c in js:
-                        z2_pass("z2_%d" % j, c, j)
-            if g == GROUPS - 2:
-                for j in range(2):
-                    sp = keep.tile([P, BANK_W], F32, name="spill_%d" % j)
-                    spill[j] = sp
-                    nc.scalar.copy(out=sp[:], in_=acc["z2_%d" % j][0][:])
+            for j in range((g + 1) * JPG):
+                for c in js:
+                    z2_pass("z2_%d" % j, c, j)
 
-        last = [6, 7]
+        xraw = rawp.tile([P, PASSES, PACK * FEAT], BF16, name="xraw", tag="raw")
+        xview = x.rearrange("(c p t) g -> p c (t g)", p=P, t=PACK)
+        for q in range(4):
+            nc.sync.dma_start(out=xraw[:, 2 * q : 2 * q + 2, :], in_=xview[:, 2 * q : 2 * q + 2, :])
+        for n in range(RAW_BUFS - 1):
+            load(n)
+        xq_codes = keep.tile([P, PASSES * FEAT], U32, name="xq_codes", align_bytes=64)
+        xq_scales = keep.tile([P, PASSES * FEAT], U8, name="xq_scales", align_bytes=64)
+        xg = [
+            grp.tile([P, 4 * FEAT * PACK], BF16, name="xg_a", tag="gv", align_bytes=64),
+            grp.tile([P, 4 * FEAT * PACK], BF16, name="xg_b", tag="gs", align_bytes=64),
+        ]
+        qw = 2 * FEAT * PACK
+        for q, engine_copy in ((0, nc.vector.tensor_copy), (2, nc.scalar.copy), (1, nc.vector.tensor_copy), (3, nc.scalar.copy)):
+            engine_copy(
+                out=xg[q // 2][:, (q % 2) * qw : (q % 2 + 1) * qw].rearrange("p (c g t) -> p c g t", c=2, t=PACK),
+                in_=xraw[:, 2 * q : 2 * q + 2, :].rearrange("p c (t g) -> p c g t", t=PACK),
+            )
+        hw = 4 * FEAT
+        load(RAW_BUFS - 1)
+        for h in range(2):
+            nc.vector.quantize_mx(
+                out=xq_codes[:, h * hw : (h + 1) * hw].bitcast(FP8X4), scales=xq_scales[:, h * hw : (h + 1) * hw], in_=xg[h][:]
+            )
+
+        LAST = CHUNKS - 1
+        for s in range(LAST):
+            regroup(s)
+            if s + RAW_BUFS < CHUNKS:
+                load(s + RAW_BUFS)
+            if s >= 1:
+                quantise(s - 1)
+                state["held"].append(s - 1)
+            g, r = divmod(s, PASSES)
+            g = g - 1
+            if g >= 0 and r == 1:
+                for j in (g * JPG, g * JPG + 1):
+                    evac_z1(nc.scalar.copy, j)
+                for j in (g * JPG, g * JPG + 1):
+                    transposes(j)
+            if g >= 0 and r == 2:
+                evac_zt(nc.scalar.copy, g * JPG)
+                evac_zt(nc.scalar.copy, g * JPG + 1)
+            if g >= 0 and r == 3:
+                quantise_z1(g * JPG)
+                quantise_z1(g * JPG + 1)
+            if g < 0 or r == 0 or r >= 2 or (r == 1 and g < 2):
+                for n in state["held"]:
+                    stream_passes(n)
+                state["held"] = []
+            if g >= 0 and r == 3:
+                group_passes(g)
+            if g == GROUPS - 2 and r == 4:
+                for j, engine_copy in ((0, nc.scalar.copy), (1, nc.vector.tensor_copy)):
+                    spill[j] = keep.tile([P, BANK_W], F32, name="spill_%d" % j)
+                    engine_copy(out=spill[j][:], in_=acc["z2_%d" % j][0][:])
+            if g < GROUPS - 2 and (r >= 3 or r == 0):
+                waiting_passes()
+            if g == GROUPS - 2 and r == 5:
+                waiting_passes(FILL_KEEP)
+
+        quantise(LAST - 1)
+        stream_passes(LAST - 1)
+        regroup_last(LAST, CUT)
+        for g in range(GROUPS - 1):
+            nc.sync.dma_start(out=out_0[0, :, g * GROUP_W : (g + 1) * GROUP_W], in_=z1sb[g][:])
+        waiting_passes(FA)
+        quantise(LAST, (0,))
+        z1_pass(PASSES - 1, 6)
+        quantise(LAST, (1,))
+        waiting_passes(FB)
+        z1_pass(PASSES - 1, 7)
+        evac_z1(nc.scalar.copy, 6)
+        waiting_passes(FC)
+        transposes(6)
+        evac_z1(nc.vector.tensor_copy, 7)
+        transposes(7)
+        nc.sync.dma_start(out=out_0[0, :, 3 * GROUP_W : 4 * GROUP_W], in_=z1sb[3][:])
+        evac_zt(nc.scalar.copy, 6)
+        quantise_z1(6)
+        evac_zt(nc.vector.tensor_copy, 7)
+        quantise_z1(7)
+        waiting_passes()
         z2sb = [rawp.tile([P, 4 * BANK_W], F32, name="z2sb_%d" % h, tag="raw") for h in range(2)]
-        order = [2, 3, 4, 5, 6, 7, 0, 1]
-        for n, j in enumerate(order):
-            key = "z2_%d" % j
-            if j < 2:
-                key = "z2b_%d" % j
-                open_group(key, "b%d" % j, 2)
-            for c in last:
-                z2_pass(key, c, j)
+        open_group("z2b_0", "b0", 2)
+        open_group("z2b_1", "b1", 2)
+        keys = {0: "z2b_0", 1: "z2b_1"}
+
+        def finish(n, j):
+            key = keys.get(j, "z2_%d" % j)
             dst = z2sb[j // 4][:, (j % 4) * BANK_W : (j % 4 + 1) * BANK_W]
             if j < 2:
                 nc.vector.tensor_tensor(out=dst, in0=acc[key][0][:], in1=spill[j][:], op=mybir.AluOpType.add)
             elif n % 2 == 0:
-                nc.vector.tensor_copy(out=dst, in_=acc[key][0][:])
-            else:
                 nc.scalar.copy(out=dst, in_=acc[key][0][:])
+            else:
+                nc.vector.tensor_copy(out=dst, in_=acc[key][0][:])
             nc.sync.dma_start(out=out_1[0, :, j * BANK_W : (j + 1) * BANK_W], in_=dst)
+
+        order = [2, 3, 4, 5, 6, 7, 0, 1]
+        for j in order[0:AHEAD]:
+            z2_pass(keys.get(j, "z2_%d" % j), 6, j)
+        for n, j in enumerate(order):
+            if n >= AHEAD:
+                z2_pass(keys.get(j, "z2_%d" % j), 6, j)
+            z2_pass(keys.get(j, "z2_%d" % j), 7, j)
+            finish(n, j)

@@ -27,6 +27,7 @@ FA = 2
 FB = 1
 FC = 1
 AHEAD = 2
+RUN = 8
 
 FLOPS = 2 * 2 * FEAT * NODES * NODES
 
@@ -68,8 +69,8 @@ def tile_graphfilter_pa_kernel(tc, x, S, out_0, out_1):
 
         def regroup_part(engine_copy, dst, src):
             engine_copy(
-                out=dst.rearrange("p (c i t) -> p c t i", i=4, t=PACK),
-                in_=src.rearrange("p t (c i) -> p c t i", i=4),
+                out=dst.rearrange("p (c i t) -> p c t i", i=RUN, t=PACK),
+                in_=src.rearrange("p t (c i) -> p c t i", i=RUN),
             )
 
         def regroup(n):

@@ -22,7 +22,7 @@ JPG = GROUP_W // BANK_W
 CHUNKS = GROUPS * PASSES
 RAW_BUFS = 4
 FILL_KEEP = 6
-CUT = 344
+CUT = 320
 FA = 2
 FB = 1
 FC = 1

@@ -220,8 +220,9 @@ def tile_graphfilter_pa_kernel(tc, x, S, out_0, out_1):
             if s + RAW_BUFS < CHUNKS:
                 load(s + RAW_BUFS)
             if s >= 1:
-                quantise(s - 1)
+                quantise(s - 1, (1,))
                 state["held"].append(s - 1)
+            quantise(s, (0,))
             g, r = divmod(s, PASSES)
             g = g - 1
             if g >= 0 and r == 1:
@@ -250,7 +251,7 @@ def tile_graphfilter_pa_kernel(tc, x, S, out_0, out_1):
             if g == GROUPS - 2 and r == 5:
                 waiting_passes(FILL_KEEP)
 
-        quantise(LAST - 1)
+        quantise(LAST - 1, (1,))
         stream_passes(LAST - 1)
         regroup_last(LAST, CUT)
         for g in range(GROUPS - 1):

@@ -22,7 +22,7 @@ JPG = GROUP_W // BANK_W
 CHUNKS = GROUPS * PASSES
 RAW_BUFS = 4
 FILL_KEEP = 6
-CUT = 320
+CUT = 240
 FA = 2
 FB = 1
 FC = 1
@@ -55,6 +55,7 @@ def tile_graphfilter_pa_kernel(tc, x, S, out_0, out_1):
         z1tg = {}
         acc = {}
         spill = {}
+        sorted_z1 = {}
 
         def load(n):
             g, c = divmod(n, PASSES)
@@ -139,6 +140,30 @@ def tile_graphfilter_pa_kernel(tc, x, S, out_0, out_1):
                     z1sb[g] = keep.tile([P, GROUP_W], F32, name="z1sb_%d" % g)
             lo = (j % JPG) * BANK_W
             engine_copy(out=z1sb[g][:, lo : lo + BANK_W], in_=acc["z1_%d" % j][0][:])
+
+        def evac_z1_sorted(engine_copy, j):
+            if "tile" not in sorted_z1:
+                sorted_z1["tile"] = rawp.tile([P, JPG, BANK_W], F32, name="z1_sorted", tag="raw")
+            engine_copy(
+                out=sorted_z1["tile"][:, j % JPG, :].rearrange("f (t p) -> f t p", t=PACK),
+                in_=acc["z1_%d" % j][0][:].rearrange("f (p t) -> f t p", t=PACK),
+            )
+
+        def unsort_z1(engine_copy, j):
+            g = j // JPG
+            if g not in z1sb:
+                z1sb[g] = rawp.tile([P, GROUP_W], F32, name="z1sb_last", tag="raw")
+            lo = (j % JPG) * BANK_W
+            engine_copy(
+                out=z1sb[g][:, lo : lo + BANK_W].rearrange("f (p t) -> f p t", t=PACK),
+                in_=sorted_z1["tile"][:, j % JPG, :].rearrange("f (t p) -> f p t", t=PACK),
+            )
+
+        def transposes_sorted(j):
+            zt = psum.tile([P, PACK, FEAT], F32, name="zt", tag="b%d" % (j % JPG))
+            zts[j] = zt
+            for t in range(PACK):
+                nc.tensor.transpose(zt[:, t, :], sorted_z1["tile"][:, j % JPG, t * P : (t + 1) * P], ident[:])
 
         def transposes(j):
             g = j // JPG
@@ -262,15 +287,17 @@ def tile_graphfilter_pa_kernel(tc, x, S, out_0, out_1):
         quantise(LAST, (1,))
         waiting_passes(FB)
         z1_pass(PASSES - 1, 7)
-        evac_z1(nc.scalar.copy, 6)
+        evac_z1_sorted(nc.scalar.copy, 6)
         waiting_passes(FC)
-        transposes(6)
-        evac_z1(nc.vector.tensor_copy, 7)
-        transposes(7)
+        transposes_sorted(6)
+        evac_z1_sorted(nc.vector.tensor_copy, 7)
+        transposes_sorted(7)
+        unsort_z1(nc.scalar.copy, 6)
+        unsort_z1(nc.vector.tensor_copy, 7)
         nc.sync.dma_start(out=out_0[0, :, 3 * GROUP_W : 4 * GROUP_W], in_=z1sb[3][:])
         evac_zt(nc.scalar.copy, 6)
         quantise_z1(6)
-        evac_zt(nc.vector.tensor_copy, 7)
+        evac_zt(nc.scalar.copy, 7)
         quantise_z1(7)
         waiting_passes()
         z2sb = [rawp.tile([P, 4 * BANK_W], F32, name="z2sb_%d" % h, tag="raw") for h in range(2)]

@@ -27,6 +27,7 @@ FA = 2
 FB = 1
 FC = 1
 AHEAD = 2
+SPLIT_LOADS = 4
 RUN = 8
 
 FLOPS = 2 * 2 * FEAT * NODES * NODES
@@ -61,12 +62,15 @@ def tile_graphfilter_pa_kernel(tc, x, S, out_0, out_1):
             g, c = divmod(n, PASSES)
             raw = rawp.tile([P, PACK, GROUP_W], BF16, name="raw", tag="raw")
             raws[n] = raw
-            nc.sync.dma_start(
-                out=raw[:],
-                in_=S[0, c * K_PASS : (c + 1) * K_PASS, g * GROUP_W : (g + 1) * GROUP_W].rearrange(
-                    "(p t) w -> p t w", t=PACK
-                ),
-            )
+            pieces = JPG if n < SPLIT_LOADS else 1
+            pw = GROUP_W // pieces
+            for i in range(pieces):
+                nc.sync.dma_start(
+                    out=raw[:, :, i * pw : (i + 1) * pw],
+                    in_=S[0, c * K_PASS : (c + 1) * K_PASS, g * GROUP_W + i * pw : g * GROUP_W + (i + 1) * pw].rearrange(
+                        "(p t) w -> p t w", t=PACK
+                    ),
+                )
 
         def regroup_part(engine_copy, dst, src):
             engine_copy(
@@ -227,7 +231,7 @@ def tile_graphfilter_pa_kernel(tc, x, S, out_0, out_1):
             grp.tile([P, 4 * FEAT * PACK], BF16, name="xg_b", tag="gs", align_bytes=64),
         ]
         qw = 2 * FEAT * PACK
-        for q, engine_copy in ((0, nc.vector.tensor_copy), (2, nc.scalar.copy), (1, nc.vector.tensor_copy), (3, nc.scalar.copy)):
+        for q, engine_copy in ((0, nc.vector.tensor_copy), (3, nc.scalar.copy), (1, nc.vector.tensor_copy), (2, nc.vector.tensor_copy)):
             engine_copy(
                 out=xg[q // 2][:, (q % 2) * qw : (q % 2 + 1) * qw].rearrange("p (c g t) -> p c g t", c=2, t=PACK),
                 in_=xraw[:, 2 * q : 2 * q + 2, :].rearrange("p c (t g) -> p c g t", t=PACK),

@@ -220,7 +220,7 @@ def tile_graphfilter_pa_kernel(tc, x, S, out_0, out_1):
 
         xraw = rawp.tile([P, PASSES, PACK * FEAT], BF16, name="xraw", tag="raw")
         xview = x.rearrange("(c p t) g -> p c (t g)", p=P, t=PACK)
-        for q in range(4):
+        for q in (0, 2, 1, 3):
             nc.sync.dma_start(out=xraw[:, 2 * q : 2 * q + 2, :], in_=xview[:, 2 * q : 2 * q + 2, :])
         for n in range(RAW_BUFS - 1):
             load(n)
@@ -231,24 +231,29 @@ def tile_graphfilter_pa_kernel(tc, x, S, out_0, out_1):
             grp.tile([P, 4 * FEAT * PACK], BF16, name="xg_b", tag="gs", align_bytes=64),
         ]
         qw = 2 * FEAT * PACK
-        for q, engine_copy in ((0, nc.vector.tensor_copy), (3, nc.scalar.copy), (1, nc.vector.tensor_copy), (2, nc.vector.tensor_copy)):
+        for q, engine_copy in ((0, nc.vector.tensor_copy), (2, nc.scalar.copy), (1, nc.vector.tensor_copy), (3, nc.scalar.copy)):
             engine_copy(
                 out=xg[q // 2][:, (q % 2) * qw : (q % 2 + 1) * qw].rearrange("p (c g t) -> p c g t", c=2, t=PACK),
                 in_=xraw[:, 2 * q : 2 * q + 2, :].rearrange("p c (t g) -> p c g t", t=PACK),
             )
         hw = 4 * FEAT
         load(RAW_BUFS - 1)
-        for h in range(2):
+
+        def quantise_x(h):
             nc.vector.quantize_mx(
                 out=xq_codes[:, h * hw : (h + 1) * hw].bitcast(FP8X4), scales=xq_scales[:, h * hw : (h + 1) * hw], in_=xg[h][:]
             )
+
+        quantise_x(0)
 
         LAST = CHUNKS - 1
         for s in range(LAST):
             regroup(s)
             if s + RAW_BUFS < CHUNKS:
                 load(s + RAW_BUFS)
-            if s >= 1:
+            if s == 0:
+                quantise_x(1)
+            else:
                 quantise(s - 1, (1,))
                 state["held"].append(s - 1)
             quantise(s, (0,))
@@ -314,6 +319,12 @@ def tile_graphfilter_pa_kernel(tc, x, S, out_0, out_1):
             dst = z2sb[j // 4][:, (j % 4) * BANK_W : (j % 4 + 1) * BANK_W]
             if j < 2:
                 nc.vector.tensor_tensor(out=dst, in0=acc[key][0][:], in1=spill[j][:], op=mybir.AluOpType.add)
+            elif n == 0:
+                hb = BANK_W // 2
+                for h in range(2):
+                    nc.scalar.copy(out=dst[:, h * hb : (h + 1) * hb], in_=acc[key][0][:, h * hb : (h + 1) * hb])
+                    nc.sync.dma_start(out=out_1[0, :, j * BANK_W + h * hb : j * BANK_W + (h + 1) * hb], in_=dst[:, h * hb : (h + 1) * hb])
+                return
             elif n % 2 == 0:
                 nc.scalar.copy(out=dst, in_=acc[key][0][:])
             else:

@@ -74,8 +74,8 @@ def tile_graphfilter_pa_kernel(tc, x, S, out_0, out_1):
 
         def regroup_part(engine_copy, dst, src):
             engine_copy(
-                out=dst.rearrange("p (c i t) -> p c t i", i=RUN, t=PACK),
-                in_=src.rearrange("p t (c i) -> p c t i", i=RUN),
+                out=dst.rearrange("p (c i u e) -> p c u i e", i=RUN, u=2, e=2),
+                in_=src.rearrange("p (u e) (c i) -> p c u i e", i=RUN, e=2),
             )
 
         def regroup(n):

from contextlib import ExitStack

import concourse.mybir as mybir
from concourse.masks import make_identity

FP8X4 = mybir.dt.float8_e4m3fn_x4
BF16 = mybir.dt.bfloat16
F32 = mybir.dt.float32
U32 = mybir.dt.uint32
U8 = mybir.dt.uint8

P = 128
NODES = 4096
FEAT = 128
PACK = 4
K_PASS = P * PACK
PASSES = NODES // K_PASS
BANK_W = 512
GROUP_W = 1024
GROUPS = NODES // GROUP_W
JPG = GROUP_W // BANK_W
CHUNKS = GROUPS * PASSES
RAW_BUFS = 4
FILL_KEEP = 6
CUT = 240
FA = 2
FB = 1
FC = 1
AHEAD = 2
SPLIT_LOADS = 4
RUN = 8

FLOPS = 2 * 2 * FEAT * NODES * NODES


def tile_graphfilter_pa_kernel(tc, x, S, out_0, out_1):
    nc = tc.nc
    with ExitStack() as ctx:
        ctx.enter_context(tc.manual_schedule())
        keep = ctx.enter_context(tc.tile_pool(name="keep", bufs=1))
        rawp = ctx.enter_context(tc.tile_pool(name="rawp", bufs=RAW_BUFS))
        grp = ctx.enter_context(tc.tile_pool(name="grp", bufs=2))
        psum = ctx.enter_context(tc.psum_pool(name="psum", bufs=1))

        ident = keep.tile([P, P], F32, name="ident")
        make_identity(nc, ident[:])

        raws = {}
        grouped = {}
        s_codes = {}
        s_scales = {}
        z1q_codes = {}
        z1q_scales = {}
        z1sb = {}
        zts = {}
        z1tg = {}
        acc = {}
        spill = {}
        sorted_z1 = {}

        def load(n):
            g, c = divmod(n, PASSES)
            raw = rawp.tile([P, PACK, GROUP_W], BF16, name="raw", tag="raw")
            raws[n] = raw
            pieces = JPG if n < SPLIT_LOADS else 1
            pw = GROUP_W // pieces
            for i in range(pieces):
                nc.sync.dma_start(
                    out=raw[:, :, i * pw : (i + 1) * pw],
                    in_=S[0, c * K_PASS : (c + 1) * K_PASS, g * GROUP_W + i * pw : g * GROUP_W + (i + 1) * pw].rearrange(
                        "(p t) w -> p t w", t=PACK
                    ),
                )

        def regroup_part(engine_copy, dst, src):
            engine_copy(
                out=dst.rearrange("p (c i u e) -> p c u i e", i=RUN, u=2, e=2),
                in_=src.rearrange("p (u e) (c i) -> p c u i e", i=RUN, e=2),
            )

        def regroup(n):
            raw = raws[n]
            gv = grp.tile([P, BANK_W * PACK], BF16, name="gv", tag="gv", align_bytes=64)
            gs = grp.tile([P, BANK_W * PACK], BF16, name="gs", tag="gs", align_bytes=64)
            grouped[n] = (gv, gs)
            regroup_part(nc.vector.tensor_copy, gv[:], raw[:, :, 0:BANK_W])
            regroup_part(nc.scalar.copy, gs[:], raw[:, :, BANK_W:GROUP_W])

        def regroup_last(n, cut):
            raw = raws[n]
            gv = grp.tile([P, BANK_W * PACK], BF16, name="gv", tag="gv", align_bytes=64)
            gs = grp.tile([P, BANK_W * PACK], BF16, name="gs", tag="gs", align_bytes=64)
            grouped[n] = (gv, gs)
            for h, dst in enumerate((gv, gs)):
                lo = h * BANK_W
                regroup_part(nc.vector.tensor_copy, dst[:, 0 : cut * PACK], raw[:, :, lo : lo + cut])
                regroup_part(nc.scalar.copy, dst[:, cut * PACK : BANK_W * PACK], raw[:, :, lo + cut : lo + BANK_W])

        def quantise(n, halves=(0, 1)):
            g, c = divmod(n, PASSES)
            if (c, g) not in s_codes:
                s_codes[(c, g)] = keep.tile([P, GROUP_W], U32, name="sc_%d_%d" % (c, g), align_bytes=64)
                s_scales[(c, g)] = keep.tile([P, GROUP_W], U8, name="ss_%d_%d" % (c, g), align_bytes=64)
            for h in halves:
                lo = h * BANK_W
                nc.vector.quantize_mx(
                    out=s_codes[(c, g)][:, lo : lo + BANK_W].bitcast(FP8X4),
                    scales=s_scales[(c, g)][:, lo : lo + BANK_W],
                    in_=grouped[n][h][:],
                )

        def open_group(key, tag, total):
            acc[key] = [psum.tile([P, BANK_W], F32, name="acc_%s" % key, tag=tag), 0, total]

        def mx_pass(key, lhs_codes, lhs_scales, c, j):
            entry = acc[key]
            g = j // JPG
            lo = (j % JPG) * BANK_W
            nc.tensor.matmul_mx(
                out=entry[0][:],
                lhsT=lhs_codes.bitcast(FP8X4),
                lhsT_scale=lhs_scales,
                rhs=s_codes[(c, g)][:, lo : lo + BANK_W].bitcast(FP8X4),
                rhs_scale=s_scales[(c, g)][:, lo : lo + BANK_W],
                start=(entry[1] == 0),
                stop=(entry[1] == entry[2] - 1),
            )
            entry[1] = entry[1] + 1

        def z1_pass(c, j):
            mx_pass("z1_%d" % j, xq_codes[:, c * FEAT : (c + 1) * FEAT], xq_scales[:, c * FEAT : (c + 1) * FEAT], c, j)

        def z2_pass(key, c, j):
            mx_pass(key, z1q_codes[c][:], z1q_scales[c][:], c, j)

        z2_tag = {0: "b4", 1: "b5", 2: "b6", 3: "b7", 4: "b2", 5: "b3", 6: "b4", 7: "b5"}

        def evac_z1(engine_copy, j):
            g = j // JPG
            if g not in z1sb:
                if g == GROUPS - 1:
                    z1sb[g] = rawp.tile([P, GROUP_W], F32, name="z1sb_last", tag="raw")
                else:
                    z1sb[g] = keep.tile([P, GROUP_W], F32, name="z1sb_%d" % g)
            lo = (j % JPG) * BANK_W
            engine_copy(out=z1sb[g][:, lo : lo + BANK_W], in_=acc["z1_%d" % j][0][:])

        def evac_z1_sorted(engine_copy, j):
            if "tile" not in sorted_z1:
                sorted_z1["tile"] = rawp.tile([P, JPG, BANK_W], F32, name="z1_sorted", tag="raw")
            engine_copy(
                out=sorted_z1["tile"][:, j % JPG, :].rearrange("f (t p) -> f t p", t=PACK),
                in_=acc["z1_%d" % j][0][:].rearrange("f (p t) -> f t p", t=PACK),
            )

        def unsort_z1(engine_copy, j):
            g = j // JPG
            if g not in z1sb:
                z1sb[g] = rawp.tile([P, GROUP_W], F32, name="z1sb_last", tag="raw")
            lo = (j % JPG) * BANK_W
            engine_copy(
                out=z1sb[g][:, lo : lo + BANK_W].rearrange("f (p t) -> f p t", t=PACK),
                in_=sorted_z1["tile"][:, j % JPG, :].rearrange("f (t p) -> f p t", t=PACK),
            )

        def transposes_sorted(j):
            zt = psum.tile([P, PACK, FEAT], F32, name="zt", tag="b%d" % (j % JPG))
            zts[j] = zt
            for t in range(PACK):
                nc.tensor.transpose(zt[:, t, :], sorted_z1["tile"][:, j % JPG, t * P : (t + 1) * P], ident[:])

        def transposes(j):
            g = j // JPG
            i = j % JPG
            zt = psum.tile([P, PACK, FEAT], F32, name="zt", tag=("b%d" % (2 + i) if g < 2 else "b%d" % i))
            zts[j] = zt
            view = z1sb[g][:, i * BANK_W : (i + 1) * BANK_W].rearrange("f (p t) -> f t p", t=PACK)
            for t in range(PACK):
                nc.tensor.transpose(zt[:, t, :], view[:, t, :], ident[:])

        def evac_zt(engine_copy, j):
            tg = keep.tile([P, FEAT * PACK], BF16, name="z1tg", tag="z1tg%d" % (j % JPG), align_bytes=64)
            z1tg[j] = tg
            engine_copy(out=tg[:].rearrange("p (f t) -> p f t", t=PACK), in_=zts[j][:].rearrange("p t f -> p f t"))

        def quantise_z1(j):
            z1q_codes[j] = keep.tile([P, FEAT], U32, name="z1qc_%d" % j, align_bytes=64)
            z1q_scales[j] = keep.tile([P, FEAT], U8, name="z1qs_%d" % j, align_bytes=64)
            nc.vector.quantize_mx(out=z1q_codes[j][:].bitcast(FP8X4), scales=z1q_scales[j][:], in_=z1tg[j][:])

        state = {"waiting": [], "held": []}

        def stream_passes(n):
            g, c = divmod(n, PASSES)
            js = [g * JPG + i for i in range(JPG)]
            if c == 0:
                for i in range(JPG):
                    open_group("z1_%d" % js[i], "b%d" % i, PASSES)
            for j in js:
                z1_pass(c, j)
            if c < g * JPG:
                for j in js:
                    state["waiting"].append((c, j))

        def waiting_passes(count=99):
            for c, j in state["waiting"][0:count]:
                if "z2_%d" % j not in acc:
                    open_group("z2_%d" % j, z2_tag[j], PASSES)
                z2_pass("z2_%d" % j, c, j)
            state["waiting"] = state["waiting"][count:]

        def group_passes(g):
            js = [g * JPG + i for i in range(JPG)]
            if g == 0:
                for j in js:
                    open_group("z2_%d" % j, z2_tag[j], 6)
            for j in range((g + 1) * JPG):
                for c in js:
                    z2_pass("z2_%d" % j, c, j)

        xraw = rawp.tile([P, PASSES, PACK * FEAT], BF16, name="xraw", tag="raw")
        xview = x.rearrange("(c p t) g -> p c (t g)", p=P, t=PACK)
        for q in (0, 2, 1, 3):
            nc.sync.dma_start(out=xraw[:, 2 * q : 2 * q + 2, :], in_=xview[:, 2 * q : 2 * q + 2, :])
        for n in range(RAW_BUFS - 1):
            load(n)
        xq_codes = keep.tile([P, PASSES * FEAT], U32, name="xq_codes", align_bytes=64)
        xq_scales = keep.tile([P, PASSES * FEAT], U8, name="xq_scales", align_bytes=64)
        xg = [
            grp.tile([P, 4 * FEAT * PACK], BF16, name="xg_a", tag="gv", align_bytes=64),
            grp.tile([P, 4 * FEAT * PACK], BF16, name="xg_b", tag="gs", align_bytes=64),
        ]
        qw = 2 * FEAT * PACK
        for q, engine_copy in ((0, nc.vector.tensor_copy), (2, nc.scalar.copy), (1, nc.vector.tensor_copy), (3, nc.scalar.copy)):
            engine_copy(
                out=xg[q // 2][:, (q % 2) * qw : (q % 2 + 1) * qw].rearrange("p (c g t) -> p c g t", c=2, t=PACK),
                in_=xraw[:, 2 * q : 2 * q + 2, :].rearrange("p c (t g) -> p c g t", t=PACK),
            )
        hw = 4 * FEAT
        load(RAW_BUFS - 1)

        def quantise_x(h):
            nc.vector.quantize_mx(
                out=xq_codes[:, h * hw : (h + 1) * hw].bitcast(FP8X4), scales=xq_scales[:, h * hw : (h + 1) * hw], in_=xg[h][:]
            )

        quantise_x(0)

        LAST = CHUNKS - 1
        for s in range(LAST):
            regroup(s)
            if s + RAW_BUFS < CHUNKS:
                load(s + RAW_BUFS)
            if s == 0:
                quantise_x(1)
            else:
                quantise(s - 1, (1,))
                state["held"].append(s - 1)
            quantise(s, (0,))
            g, r = divmod(s, PASSES)
            g = g - 1
            if g >= 0 and r == 1:
                for j in (g * JPG, g * JPG + 1):
                    evac_z1(nc.scalar.copy, j)
                for j in (g * JPG, g * JPG + 1):
                    transposes(j)
            if g >= 0 and r == 2:
                evac_zt(nc.scalar.copy, g * JPG)
                evac_zt(nc.scalar.copy, g * JPG + 1)
            if g >= 0 and r == 3:
                quantise_z1(g * JPG)
                quantise_z1(g * JPG + 1)
            if g < 0 or r == 0 or r >= 2 or (r == 1 and g < 2):
                for n in state["held"]:
                    stream_passes(n)
                state["held"] = []
            if g >= 0 and r == 3:
                group_passes(g)
            if g == GROUPS - 2 and r == 4:
                for j, engine_copy in ((0, nc.scalar.copy), (1, nc.vector.tensor_copy)):
                    spill[j] = keep.tile([P, BANK_W], F32, name="spill_%d" % j)
                    engine_copy(out=spill[j][:], in_=acc["z2_%d" % j][0][:])
            if g < GROUPS - 2 and (r >= 3 or r == 0):
                waiting_passes()
            if g == GROUPS - 2 and r == 5:
                waiting_passes(FILL_KEEP)

        quantise(LAST - 1, (1,))
        stream_passes(LAST - 1)
        regroup_last(LAST, CUT)
        for g in range(GROUPS - 1):
            nc.sync.dma_start(out=out_0[0, :, g * GROUP_W : (g + 1) * GROUP_W], in_=z1sb[g][:])
        waiting_passes(FA)
        quantise(LAST, (0,))
        z1_pass(PASSES - 1, 6)
        quantise(LAST, (1,))
        waiting_passes(FB)
        z1_pass(PASSES - 1, 7)
        evac_z1_sorted(nc.scalar.copy, 6)
        waiting_passes(FC)
        transposes_sorted(6)
        evac_z1_sorted(nc.vector.tensor_copy, 7)
        transposes_sorted(7)
        unsort_z1(nc.scalar.copy, 6)
        unsort_z1(nc.vector.tensor_copy, 7)
        nc.sync.dma_start(out=out_0[0, :, 3 * GROUP_W : 4 * GROUP_W], in_=z1sb[3][:])
        evac_zt(nc.scalar.copy, 6)
        quantise_z1(6)
        evac_zt(nc.scalar.copy, 7)
        quantise_z1(7)
        waiting_passes()
        z2sb = [rawp.tile([P, 4 * BANK_W], F32, name="z2sb_%d" % h, tag="raw") for h in range(2)]
        open_group("z2b_0", "b0", 2)
        open_group("z2b_1", "b1", 2)
        keys = {0: "z2b_0", 1: "z2b_1"}

        def finish(n, j):
            key = keys.get(j, "z2_%d" % j)
            dst = z2sb[j // 4][:, (j % 4) * BANK_W : (j % 4 + 1) * BANK_W]
            if j < 2:
                nc.vector.tensor_tensor(out=dst, in0=acc[key][0][:], in1=spill[j][:], op=mybir.AluOpType.add)
            elif n == 0:
                hb = BANK_W // 2
                for h in range(2):
                    nc.scalar.copy(out=dst[:, h * hb : (h + 1) * hb], in_=acc[key][0][:, h * hb : (h + 1) * hb])
                    nc.sync.dma_start(out=out_1[0, :, j * BANK_W + h * hb : j * BANK_W + (h + 1) * hb], in_=dst[:, h * hb : (h + 1) * hb])
                return
            elif n % 2 == 0:
                nc.scalar.copy(out=dst, in_=acc[key][0][:])
            else:
                nc.vector.tensor_copy(out=dst, in_=acc[key][0][:])
            nc.sync.dma_start(out=out_1[0, :, j * BANK_W : (j + 1) * BANK_W], in_=dst)

        order = [2, 3, 4, 5, 6, 7, 0, 1]
        for j in order[0:AHEAD]:
            z2_pass(keys.get(j, "z2_%d" % j), 6, j)
        for n, j in enumerate(order):
            if n >= AHEAD:
                z2_pass(keys.get(j, "z2_%d" % j), 6, j)
            z2_pass(keys.get(j, "z2_%d" % j), 7, j)
            finish(n, j)
